import numpy as np
import ml_dtypes


def mxq(x, axis, fmt="e4m3"):
    dtype, down = {"e4m3": (ml_dtypes.float8_e4m3fn, 7), "e5m2": (ml_dtypes.float8_e5m2, 14)}[fmt]
    v = np.moveaxis(np.asarray(x, np.float32).astype(ml_dtypes.bfloat16).astype(np.float64), axis, -1)
    blocks = v.reshape(v.shape[:-1] + (-1, 32))
    amax = np.abs(blocks).max(-1, keepdims=True)
    byte = np.maximum(np.where(amax > 0, np.frexp(amax)[1] - 1 + 127, 0) - down, 1)
    scale = np.exp2(byte - 127.0)
    codes = (blocks / scale).astype(np.float32).astype(dtype).astype(np.float64)
    return np.moveaxis((codes * scale).reshape(v.shape), -1, axis)


WIDE = False


def mx_kscale(k):
    if not WIDE:
        return np.ones(k)
    levels = np.array([10, -10, 5, -5, 0])
    a = np.random.permutation(np.resize(levels, k // 512 * 4)).reshape(k // 512, 4)
    idx = np.arange(k)
    return np.exp2(a[idx // 512, idx % 128 // 32])


BF16 = ml_dtypes.bfloat16


def bf(x):
    return np.asarray(x, np.float32).astype(BF16)


def f64(x):
    return np.asarray(x).astype(np.float64)


B, N, DIM, HEADS, WIN, FF, TIME_DIM = 4, 1024, 512, 4, 512, 2048, 512
HD = DIM // HEADS
EPS = 1e-5


def layernorm(x, g, b):
    mu = x.mean(-1, keepdims=True)
    var = np.square(x - mu).mean(-1, keepdims=True)
    return (x - mu) / np.sqrt(var + EPS) * g + b


def setup_inputs():
    s = mx_kscale(DIM)
    return {
        "x": bf(np.random.standard_normal((B, N, DIM)) * (0.5 + 1.5 * np.random.random((B, N, 1))) + 0.5 * np.random.standard_normal((B, N, 1))),
        "t_scale": bf(np.random.standard_normal((B, DIM)) * 0.5),
        "t_shift": bf(np.random.standard_normal((B, DIM)) * 0.5 * s),
        "ln1_g": bf((1.0 + 0.1 * np.random.standard_normal(DIM)) * s),
        "ln1_b": bf(0.1 * np.random.standard_normal(DIM) * s),
        "qkv_w": bf(np.random.standard_normal((DIM, 3 * DIM)) * 1.2 / np.sqrt(DIM) / s[:, None]),
        "qkv_b": bf(np.random.standard_normal(3 * DIM) * 0.2),
    }


def reference(x, t_scale, t_shift, ln1_g, ln1_b, qkv_w, qkv_b):
    x_norm = layernorm(f64(x), f64(ln1_g), f64(ln1_b)) * (1.0 + f64(t_scale)[:, None, :]) + f64(t_shift)[:, None, :]
    qkv = (mxq(x_norm, 2, "e4m3") @ mxq(f64(qkv_w), 0, "e4m3")) + f64(qkv_b)
    return qkv.reshape(B, N, 3, HEADS, HD).transpose(2, 0, 3, 1, 4)

@@ -1,0 +1,229 @@
+from contextlib import ExitStack
+
+import concourse.mybir as mybir
+from concourse.masks import make_identity
+
+F32 = mybir.dt.float32
+BF16 = mybir.dt.bfloat16
+U32 = mybir.dt.uint32
+U8 = mybir.dt.uint8
+FP8X4 = mybir.dt.float8_e4m3fn_x4
+ACT = mybir.ActivationFunctionType
+ALU = mybir.AluOpType
+
+P = 128
+PACK = 4
+BATCH, TOKENS, DIM = 4, 1024, 512
+PROJ, HEADS, HEAD_DIM = 3, 4, 128
+PROJ_COLS = HEADS * HEAD_DIM
+OUT_COLS = PROJ * PROJ_COLS
+TILES = 4
+BLOCK = TILES * P
+BLOCKS_PER_BATCH = TOKENS // BLOCK
+N_BLOCKS = BATCH * BLOCKS_PER_BATCH
+EPS = 1e-5
+
+assert DIM == P * PACK
+
+FLOPS = 2 * BATCH * TOKENS * DIM * OUT_COLS
+
+
+def tile_localattentionblock_pa_t_kernel(
+    tc, x, t_scale, t_shift, ln1_g, ln1_b, qkv_w, qkv_b, out
+):
+    nc = tc.nc
+    with ExitStack() as ctx:
+        const = ctx.enter_context(tc.tile_pool(name="const", bufs=1))
+        rows = ctx.enter_context(tc.tile_pool(name="rows", bufs=1))
+        small = ctx.enter_context(tc.tile_pool(name="small", bufs=3))
+        work = ctx.enter_context(tc.tile_pool(name="work", bufs=2))
+        results = ctx.enter_context(tc.tile_pool(name="results", bufs=6))
+        psum_t = ctx.enter_context(tc.psum_pool(name="psum_t", bufs=1))
+        psum_acc = ctx.enter_context(tc.psum_pool(name="psum_acc", bufs=4))
+        ctx.enter_context(tc.manual_schedule())
+
+        def load_block(blk):
+            b, half = divmod(blk, BLOCKS_PER_BATCH)
+            x_blk = rows.tile([P, TILES, DIM], BF16, name="x_blk%d" % blk)
+            nc.sync.dma_start(
+                out=x_blk[:],
+                in_=x[b, half * BLOCK : (half + 1) * BLOCK, :].rearrange(
+                    "(p i) k -> p i k", i=TILES
+                ),
+            )
+            return x_blk
+
+        x_blocks = [load_block(0)]
+        w_rows = const.tile([P, PACK, OUT_COLS], BF16)
+        nc.sync.dma_start(out=w_rows[:], in_=qkv_w.rearrange("(p t) c -> p t c", t=PACK))
+        for blk in range(1, N_BLOCKS):
+            x_blocks.append(load_block(blk))
+
+        ln_gain = const.tile([P, PACK], BF16)
+        ln_shift = const.tile([P, PACK], BF16)
+        time_scale = const.tile([P, BATCH, PACK], BF16)
+        time_shift = const.tile([P, BATCH, PACK], BF16)
+        nc.scalar.dma_start(out=ln_gain[:], in_=ln1_g.rearrange("(p t) -> p t", t=PACK))
+        nc.scalar.dma_start(out=ln_shift[:], in_=ln1_b.rearrange("(p t) -> p t", t=PACK))
+        nc.scalar.dma_start(out=time_scale[:], in_=t_scale.rearrange("b (p t) -> p b t", t=PACK))
+        nc.scalar.dma_start(out=time_shift[:], in_=t_shift.rearrange("b (p t) -> p b t", t=PACK))
+        bias_rows = const.tile([P, OUT_COLS], BF16)
+        nc.scalar.dma_start(out=bias_rows[:], in_=qkv_b.partition_broadcast(P))
+
+        ident = const.tile([P, P], F32)
+        make_identity(nc, ident[:])
+        eps = const.tile([P, 1], F32)
+        nc.vector.memset(eps[:], EPS)
+
+        one_plus = const.tile([P, BATCH, PACK], F32)
+        mod_gain = const.tile([P, BATCH, PACK], F32)
+        mod_shift = const.tile([P, BATCH, PACK], F32)
+        per_batch = [P, BATCH, PACK]
+        nc.vector.tensor_scalar_add(out=one_plus[:], in0=time_scale[:], scalar1=1.0)
+        nc.vector.tensor_mul(
+            out=mod_gain[:], in0=one_plus[:], in1=ln_gain[:].unsqueeze(1).to_broadcast(per_batch)
+        )
+        nc.vector.tensor_mul(
+            out=mod_shift[:], in0=one_plus[:], in1=ln_shift[:].unsqueeze(1).to_broadcast(per_batch)
+        )
+        nc.vector.tensor_add(out=mod_shift[:], in0=mod_shift[:], in1=time_shift[:])
+
+        w_grouped = const.tile([P, OUT_COLS, PACK], BF16, align_bytes=64)
+        w_words = const.tile([P, OUT_COLS], U32, align_bytes=64)
+        w_scales = const.tile([P, OUT_COLS], U8, align_bytes=64)
+
+        def quantise_weights():
+            for j in range(PROJ):
+                cols = slice(j * PROJ_COLS, (j + 1) * PROJ_COLS)
+                nc.vector.tensor_copy(
+                    out=w_grouped[:, cols, :], in_=w_rows[:, :, cols].rearrange("p t c -> p c t")
+                )
+            for j in range(PROJ):
+                cols = slice(j * PROJ_COLS, (j + 1) * PROJ_COLS)
+                nc.vector.quantize_mx(
+                    out=w_words[:, cols].bitcast(FP8X4),
+                    scales=w_scales[:, cols],
+                    in_=w_grouped[:, cols, :].rearrange("p c t -> p (c t)"),
+                )
+
+        neg_means, rstds, xhats, banks, planes, grouped, words, scales = {}, {}, {}, {}, {}, {}, {}, {}
+
+        def statistics(blk):
+            x_blk = x_blocks[blk]
+            unread = work.tile([P, TILES, DIM], BF16, name="unread")
+            total = small.tile([P, TILES], F32, name="total")
+            spread = small.tile([P, TILES], F32, name="spread")
+            neg_means[blk] = small.tile([P, TILES], F32, name="neg_mean")
+            rstds[blk] = small.tile([P, TILES], F32, name="rstd")
+            for i in range(TILES):
+                nc.scalar.activation(
+                    out=unread[:, i, :], in_=x_blk[:, i, :], func=ACT.Identity,
+                    accum_out=total[:, i : i + 1],
+                )
+            nc.scalar.mul(out=neg_means[blk][:], in_=total[:], mul=-1.0 / DIM)
+            for i in range(TILES):
+                nc.scalar.activation(
+                    out=unread[:, i, :], in_=x_blk[:, i, :], func=ACT.Square,
+                    bias=neg_means[blk][:, i : i + 1], accum_out=spread[:, i : i + 1],
+                )
+            nc.scalar.activation(
+                out=rstds[blk][:], in_=spread[:], func=ACT.Abs_reciprocal_sqrt,
+                scale=1.0 / DIM, bias=eps[:],
+            )
+
+        def normalise(blk):
+            xhats[blk] = work.tile([P, TILES, PACK, P], F32, name="xhat")
+            for i in range(TILES):
+                nc.gpsimd.tensor_scalar(
+                    out=xhats[blk][:, i, :, :],
+                    in0=x_blocks[blk][:, i, :].rearrange("n (p t) -> n t p", t=PACK),
+                    scalar1=neg_means[blk][:, i : i + 1], scalar2=rstds[blk][:, i : i + 1],
+                    op0=ALU.add, op1=ALU.mult,
+                )
+
+        def transpose(blk):
+            banks[blk] = [psum_t.tile([P, BLOCK], F32, name="xhat_t%d" % t) for t in range(PACK)]
+            for i in range(TILES):
+                for t in range(PACK):
+                    nc.tensor.transpose(
+                        out=banks[blk][t][:, i * P : (i + 1) * P], in_=xhats[blk][:, i, t, :],
+                        identity=ident[:],
+                    )
+
+        def modulate(blk):
+            b = blk // BLOCKS_PER_BATCH
+            planes[blk] = work.tile([P, PACK, BLOCK], BF16, name="planes")
+            for t in range(PACK):
+                nc.scalar.activation(
+                    out=planes[blk][:, t, :], in_=banks[blk][t][:], func=ACT.Identity,
+                    scale=mod_gain[:, b, t : t + 1], bias=mod_shift[:, b, t : t + 1],
+                )
+
+        def regroup(blk):
+            grouped[blk] = work.tile([P, BLOCK, PACK], BF16, name="grouped", align_bytes=64)
+            nc.gpsimd.tensor_scalar(
+                out=grouped[blk][:], in0=planes[blk][:].rearrange("p t n -> p n t"),
+                scalar1=1.0, scalar2=0.0, op0=ALU.mult, op1=ALU.add,
+            )
+
+        def quantise(blk):
+            words[blk] = work.tile([P, BLOCK], U32, name="words", align_bytes=64)
+            scales[blk] = work.tile([P, BLOCK], U8, name="scales", align_bytes=64)
+            nc.vector.quantize_mx(
+                out=words[blk][:].bitcast(FP8X4), scales=scales[blk][:],
+                in_=grouped[blk][:].rearrange("p n t -> p (n t)"),
+            )
+
+        def project(blk, j):
+            b, half = divmod(blk, BLOCKS_PER_BATCH)
+            cols = slice(j * PROJ_COLS, (j + 1) * PROJ_COLS)
+            result = results.tile([P, HEADS, TILES, HEAD_DIM], F32, name="result")
+            for i in range(TILES):
+                tokens = slice(i * P, (i + 1) * P)
+                acc = psum_acc.tile([P, PROJ_COLS], F32, name="acc")
+                nc.tensor.matmul_mx(
+                    out=acc[:],
+                    lhsT=words[blk][:, tokens].bitcast(FP8X4), lhsT_scale=scales[blk][:, tokens],
+                    rhs=w_words[:, cols].bitcast(FP8X4), rhs_scale=w_scales[:, cols],
+                    start=True, stop=True,
+                )
+                nc.vector.tensor_tensor(
+                    out=result[:, :, i, :],
+                    in0=acc[:].rearrange("p (h d) -> p h d", h=HEADS),
+                    in1=bias_rows[:, cols].rearrange("p (h d) -> p h d", h=HEADS),
+                    op=ALU.add,
+                )
+            nc.sync.dma_start(
+                out=out[j, b, :, half * BLOCK : (half + 1) * BLOCK, :].rearrange(
+                    "h (p i) d -> p h i d", i=TILES
+                ),
+                in_=result[:],
+            )
+
+        statistics(0)
+        normalise(0)
+        transpose(0)
+        statistics(1)
+        normalise(1)
+        modulate(0)
+        regroup(0)
+        quantise_weights()
+        quantise(0)
+        transpose(1)
+
+        for blk in range(N_BLOCKS):
+            if blk + 2 < N_BLOCKS:
+                statistics(blk + 2)
+            if blk + 1 < N_BLOCKS:
+                modulate(blk + 1)
+            if blk + 2 < N_BLOCKS:
+                normalise(blk + 2)
+            if blk + 1 < N_BLOCKS:
+                regroup(blk + 1)
+            project(blk, 0)
+            project(blk, 1)
+            if blk + 2 < N_BLOCKS:
+                transpose(blk + 2)
+            if blk + 1 < N_BLOCKS:
+                quantise(blk + 1)
+            project(blk, 2)

@@ -19,8 +19,12 @@ PROJ_COLS = HEADS * HEAD_DIM
 OUT_COLS = PROJ * PROJ_COLS
 TILES = 4
 BLOCK = TILES * P
+PAIR = 2
+PAIR_TOKENS = PAIR * P
+PAIRS_PER_BLOCK = TILES // PAIR
 BLOCKS_PER_BATCH = TOKENS // BLOCK
 N_BLOCKS = BATCH * BLOCKS_PER_BATCH
+N_PAIRS = N_BLOCKS * PAIRS_PER_BLOCK
 EPS = 1e-5
 
 assert DIM == P * PACK
@@ -35,10 +39,11 @@ def tile_localattentionblock_pa_t_kernel(
     with ExitStack() as ctx:
         const = ctx.enter_context(tc.tile_pool(name="const", bufs=1))
         rows = ctx.enter_context(tc.tile_pool(name="rows", bufs=1))
-        small = ctx.enter_context(tc.tile_pool(name="small", bufs=3))
+        small = ctx.enter_context(tc.tile_pool(name="small", bufs=4))
         work = ctx.enter_context(tc.tile_pool(name="work", bufs=2))
+        packed = ctx.enter_context(tc.tile_pool(name="packed", bufs=2 * PAIRS_PER_BLOCK))
         results = ctx.enter_context(tc.tile_pool(name="results", bufs=6))
-        psum_t = ctx.enter_context(tc.psum_pool(name="psum_t", bufs=1))
+        psum_t = ctx.enter_context(tc.psum_pool(name="psum_t", bufs=2))
         psum_acc = ctx.enter_context(tc.psum_pool(name="psum_acc", bufs=4))
         ctx.enter_context(tc.manual_schedule())
 
@@ -108,70 +113,77 @@ def tile_localattentionblock_pa_t_kernel(
 
         neg_means, rstds, xhats, banks, planes, grouped, words, scales = {}, {}, {}, {}, {}, {}, {}, {}
 
-        def statistics(blk):
-            x_blk = x_blocks[blk]
-            unread = work.tile([P, TILES, DIM], BF16, name="unread")
-            total = small.tile([P, TILES], F32, name="total")
-            spread = small.tile([P, TILES], F32, name="spread")
-            neg_means[blk] = small.tile([P, TILES], F32, name="neg_mean")
-            rstds[blk] = small.tile([P, TILES], F32, name="rstd")
-            for i in range(TILES):
+        def pair_rows(pair):
+            blk, part = divmod(pair, PAIRS_PER_BLOCK)
+            return x_blocks[blk][:, part * PAIR : (part + 1) * PAIR, :]
+
+        def statistics(pair):
+            x_pair = pair_rows(pair)
+            unread = work.tile([P, PAIR, DIM], BF16, name="unread")
+            total = small.tile([P, PAIR], F32, name="total")
+            spread = small.tile([P, PAIR], F32, name="spread")
+            neg_means[pair] = small.tile([P, PAIR], F32, name="neg_mean")
+            rstds[pair] = small.tile([P, PAIR], F32, name="rstd")
+            for i in range(PAIR):
                 nc.scalar.activation(
-                    out=unread[:, i, :], in_=x_blk[:, i, :], func=ACT.Identity,
+                    out=unread[:, i, :], in_=x_pair[:, i, :], func=ACT.Identity,
                     accum_out=total[:, i : i + 1],
                 )
-            nc.scalar.mul(out=neg_means[blk][:], in_=total[:], mul=-1.0 / DIM)
-            for i in range(TILES):
+            nc.scalar.mul(out=neg_means[pair][:], in_=total[:], mul=-1.0 / DIM)
+            for i in range(PAIR):
                 nc.scalar.activation(
-                    out=unread[:, i, :], in_=x_blk[:, i, :], func=ACT.Square,
-                    bias=neg_means[blk][:, i : i + 1], accum_out=spread[:, i : i + 1],
+                    out=unread[:, i, :], in_=x_pair[:, i, :], func=ACT.Square,
+                    bias=neg_means[pair][:, i : i + 1], accum_out=spread[:, i : i + 1],
                 )
             nc.scalar.activation(
-                out=rstds[blk][:], in_=spread[:], func=ACT.Abs_reciprocal_sqrt,
+                out=rstds[pair][:], in_=spread[:], func=ACT.Abs_reciprocal_sqrt,
                 scale=1.0 / DIM, bias=eps[:],
             )
 
-        def normalise(blk):
-            xhats[blk] = work.tile([P, TILES, PACK, P], F32, name="xhat")
-            for i in range(TILES):
+        def normalise(pair):
+            x_pair = pair_rows(pair)
+            xhats[pair] = work.tile([P, PAIR, PACK, P], F32, name="xhat")
+            for i in range(PAIR):
                 nc.gpsimd.tensor_scalar(
-                    out=xhats[blk][:, i, :, :],
-                    in0=x_blocks[blk][:, i, :].rearrange("n (p t) -> n t p", t=PACK),
-                    scalar1=neg_means[blk][:, i : i + 1], scalar2=rstds[blk][:, i : i + 1],
+                    out=xhats[pair][:, i, :, :],
+                    in0=x_pair[:, i, :].rearrange("n (p t) -> n t p", t=PACK),
+                    scalar1=neg_means[pair][:, i : i + 1], scalar2=rstds[pair][:, i : i + 1],
                     op0=ALU.add, op1=ALU.mult,
                 )
 
-        def transpose(blk):
-            banks[blk] = [psum_t.tile([P, BLOCK], F32, name="xhat_t%d" % t) for t in range(PACK)]
-            for i in range(TILES):
+        def transpose(pair):
+            banks[pair] = [
+                psum_t.tile([P, PACK // 2, PAIR_TOKENS], F32, name="xhat_t%d" % u) for u in range(2)
+            ]
+            for i in range(PAIR):
                 for t in range(PACK):
                     nc.tensor.transpose(
-                        out=banks[blk][t][:, i * P : (i + 1) * P], in_=xhats[blk][:, i, t, :],
-                        identity=ident[:],
+                        out=banks[pair][t // 2][:, t % 2, i * P : (i + 1) * P],
+                        in_=xhats[pair][:, i, t, :], identity=ident[:],
                     )
 
-        def modulate(blk):
-            b = blk // BLOCKS_PER_BATCH
-            planes[blk] = work.tile([P, PACK, BLOCK], BF16, name="planes")
+        def modulate(pair):
+            b = pair // (PAIRS_PER_BLOCK * BLOCKS_PER_BATCH)
+            planes[pair] = work.tile([P, PACK, PAIR_TOKENS], BF16, name="planes")
             for t in range(PACK):
                 nc.scalar.activation(
-                    out=planes[blk][:, t, :], in_=banks[blk][t][:], func=ACT.Identity,
+                    out=planes[pair][:, t, :], in_=banks[pair][t // 2][:, t % 2, :], func=ACT.Identity,
                     scale=mod_gain[:, b, t : t + 1], bias=mod_shift[:, b, t : t + 1],
                 )
 
-        def regroup(blk):
-            grouped[blk] = work.tile([P, BLOCK, PACK], BF16, name="grouped", align_bytes=64)
+        def regroup(pair):
+            grouped[pair] = work.tile([P, PAIR_TOKENS, PACK], BF16, name="grouped", align_bytes=64)
             nc.gpsimd.tensor_scalar(
-                out=grouped[blk][:], in0=planes[blk][:].rearrange("p t n -> p n t"),
+                out=grouped[pair][:], in0=planes[pair][:].rearrange("p t n -> p n t"),
                 scalar1=1.0, scalar2=0.0, op0=ALU.mult, op1=ALU.add,
             )
 
-        def quantise(blk):
-            words[blk] = work.tile([P, BLOCK], U32, name="words", align_bytes=64)
-            scales[blk] = work.tile([P, BLOCK], U8, name="scales", align_bytes=64)
+        def quantise(pair):
+            words[pair] = packed.tile([P, PAIR_TOKENS], U32, name="words", align_bytes=64)
+            scales[pair] = packed.tile([P, PAIR_TOKENS], U8, name="scales", align_bytes=64)
             nc.vector.quantize_mx(
-                out=words[blk][:].bitcast(FP8X4), scales=scales[blk][:],
-                in_=grouped[blk][:].rearrange("p n t -> p (n t)"),
+                out=words[pair][:].bitcast(FP8X4), scales=scales[pair][:],
+                in_=grouped[pair][:].rearrange("p n t -> p (n t)"),
             )
 
         def project(blk, j):
@@ -179,11 +191,12 @@ def tile_localattentionblock_pa_t_kernel(
             cols = slice(j * PROJ_COLS, (j + 1) * PROJ_COLS)
             result = results.tile([P, HEADS, TILES, HEAD_DIM], F32, name="result")
             for i in range(TILES):
-                tokens = slice(i * P, (i + 1) * P)
+                pair = blk * PAIRS_PER_BLOCK + i // PAIR
+                tokens = slice((i % PAIR) * P, (i % PAIR + 1) * P)
                 acc = psum_acc.tile([P, PROJ_COLS], F32, name="acc")
                 nc.tensor.matmul_mx(
                     out=acc[:],
-                    lhsT=words[blk][:, tokens].bitcast(FP8X4), lhsT_scale=scales[blk][:, tokens],
+                    lhsT=words[pair][:, tokens].bitcast(FP8X4), lhsT_scale=scales[pair][:, tokens],
                     rhs=w_words[:, cols].bitcast(FP8X4), rhs_scale=w_scales[:, cols],
                     start=True, stop=True,
                 )
@@ -200,6 +213,16 @@ def tile_localattentionblock_pa_t_kernel(
                 in_=result[:],
             )
 
+        def when_there(stage, pair):
+            if pair < N_PAIRS:
+                stage(pair)
+
+        def norm_step(pair):
+            when_there(statistics, pair + 2)
+            when_there(modulate, pair + 1)
+            when_there(normalise, pair + 2)
+            when_there(regroup, pair + 1)
+
         statistics(0)
         normalise(0)
         transpose(0)
@@ -210,20 +233,18 @@ def tile_localattentionblock_pa_t_kernel(
         quantise_weights()
         quantise(0)
         transpose(1)
+        norm_step(0)
+        quantise(1)
+        transpose(2)
 
         for blk in range(N_BLOCKS):
-            if blk + 2 < N_BLOCKS:
-                statistics(blk + 2)
-            if blk + 1 < N_BLOCKS:
-                modulate(blk + 1)
-            if blk + 2 < N_BLOCKS:
-                normalise(blk + 2)
-            if blk + 1 < N_BLOCKS:
-                regroup(blk + 1)
+            first = blk * PAIRS_PER_BLOCK
+            norm_step(first + 1)
             project(blk, 0)
+            when_there(transpose, first + 3)
+            norm_step(first + 2)
             project(blk, 1)
-            if blk + 2 < N_BLOCKS:
-                transpose(blk + 2)
-            if blk + 1 < N_BLOCKS:
-                quantise(blk + 1)
+            when_there(quantise, first + 2)
             project(blk, 2)
+            when_there(transpose, first + 4)
+            when_there(quantise, first + 3)

@@ -19,12 +19,9 @@ PROJ_COLS = HEADS * HEAD_DIM
 OUT_COLS = PROJ * PROJ_COLS
 TILES = 4
 BLOCK = TILES * P
-PAIR = 2
-PAIR_TOKENS = PAIR * P
-PAIRS_PER_BLOCK = TILES // PAIR
 BLOCKS_PER_BATCH = TOKENS // BLOCK
 N_BLOCKS = BATCH * BLOCKS_PER_BATCH
-N_PAIRS = N_BLOCKS * PAIRS_PER_BLOCK
+HEAD_BLOCKS = 3
 EPS = 1e-5
 
 assert DIM == P * PACK
@@ -41,9 +38,8 @@ def tile_localattentionblock_pa_t_kernel(
         rows = ctx.enter_context(tc.tile_pool(name="rows", bufs=1))
         small = ctx.enter_context(tc.tile_pool(name="small", bufs=4))
         work = ctx.enter_context(tc.tile_pool(name="work", bufs=2))
-        packed = ctx.enter_context(tc.tile_pool(name="packed", bufs=2 * PAIRS_PER_BLOCK))
         results = ctx.enter_context(tc.tile_pool(name="results", bufs=6))
-        psum_t = ctx.enter_context(tc.psum_pool(name="psum_t", bufs=2))
+        psum_t = ctx.enter_context(tc.psum_pool(name="psum_t", bufs=1))
         psum_acc = ctx.enter_context(tc.psum_pool(name="psum_acc", bufs=4))
         ctx.enter_context(tc.manual_schedule())
 
@@ -58,10 +54,10 @@ def tile_localattentionblock_pa_t_kernel(
             )
             return x_blk
 
-        x_blocks = [load_block(0)]
+        x_blocks = [load_block(blk) for blk in range(HEAD_BLOCKS)]
         w_rows = const.tile([P, PACK, OUT_COLS], BF16)
         nc.sync.dma_start(out=w_rows[:], in_=qkv_w.rearrange("(p t) c -> p t c", t=PACK))
-        for blk in range(1, N_BLOCKS):
+        for blk in range(HEAD_BLOCKS, N_BLOCKS):
             x_blocks.append(load_block(blk))
 
         ln_gain = const.tile([P, PACK], BF16)
@@ -83,15 +79,17 @@ def tile_localattentionblock_pa_t_kernel(
         one_plus = const.tile([P, BATCH, PACK], F32)
         mod_gain = const.tile([P, BATCH, PACK], F32)
         mod_shift = const.tile([P, BATCH, PACK], F32)
-        per_batch = [P, BATCH, PACK]
-        nc.vector.tensor_scalar_add(out=one_plus[:], in0=time_scale[:], scalar1=1.0)
-        nc.vector.tensor_mul(
-            out=mod_gain[:], in0=one_plus[:], in1=ln_gain[:].unsqueeze(1).to_broadcast(per_batch)
-        )
-        nc.vector.tensor_mul(
-            out=mod_shift[:], in0=one_plus[:], in1=ln_shift[:].unsqueeze(1).to_broadcast(per_batch)
-        )
-        nc.vector.tensor_add(out=mod_shift[:], in0=mod_shift[:], in1=time_shift[:])
+
+        def fold_modulation():
+            per_batch = [P, BATCH, PACK]
+            nc.vector.tensor_scalar_add(out=one_plus[:], in0=time_scale[:], scalar1=1.0)
+            nc.vector.tensor_mul(
+                out=mod_gain[:], in0=one_plus[:], in1=ln_gain[:].unsqueeze(1).to_broadcast(per_batch)
+            )
+            nc.vector.tensor_mul(
+                out=mod_shift[:], in0=one_plus[:], in1=ln_shift[:].unsqueeze(1).to_broadcast(per_batch)
+            )
+            nc.vector.tensor_add(out=mod_shift[:], in0=mod_shift[:], in1=time_shift[:])
 
         w_grouped = const.tile([P, OUT_COLS, PACK], BF16, align_bytes=64)
         w_words = const.tile([P, OUT_COLS], U32, align_bytes=64)
@@ -113,77 +111,83 @@ def tile_localattentionblock_pa_t_kernel(
 
         neg_means, rstds, xhats, banks, planes, grouped, words, scales = {}, {}, {}, {}, {}, {}, {}, {}
 
-        def pair_rows(pair):
-            blk, part = divmod(pair, PAIRS_PER_BLOCK)
-            return x_blocks[blk][:, part * PAIR : (part + 1) * PAIR, :]
-
-        def statistics(pair):
-            x_pair = pair_rows(pair)
-            unread = work.tile([P, PAIR, DIM], BF16, name="unread")
-            total = small.tile([P, PAIR], F32, name="total")
-            spread = small.tile([P, PAIR], F32, name="spread")
-            neg_means[pair] = small.tile([P, PAIR], F32, name="neg_mean")
-            rstds[pair] = small.tile([P, PAIR], F32, name="rstd")
-            for i in range(PAIR):
+        def statistics(blk):
+            x_blk = x_blocks[blk]
+            unread = work.tile([P, TILES, DIM], BF16, name="unread")
+            total = small.tile([P, TILES], F32, name="total")
+            spread = small.tile([P, TILES], F32, name="spread")
+            neg_means[blk] = small.tile([P, TILES], F32, name="neg_mean")
+            rstds[blk] = small.tile([P, TILES], F32, name="rstd")
+            for i in range(TILES):
                 nc.scalar.activation(
-                    out=unread[:, i, :], in_=x_pair[:, i, :], func=ACT.Identity,
+                    out=unread[:, i, :], in_=x_blk[:, i, :], func=ACT.Identity,
                     accum_out=total[:, i : i + 1],
                 )
-            nc.scalar.mul(out=neg_means[pair][:], in_=total[:], mul=-1.0 / DIM)
-            for i in range(PAIR):
+            nc.scalar.mul(out=neg_means[blk][:], in_=total[:], mul=-1.0 / DIM)
+            for i in range(TILES):
                 nc.scalar.activation(
-                    out=unread[:, i, :], in_=x_pair[:, i, :], func=ACT.Square,
-                    bias=neg_means[pair][:, i : i + 1], accum_out=spread[:, i : i + 1],
+                    out=unread[:, i, :], in_=x_blk[:, i, :], func=ACT.Square,
+                    bias=neg_means[blk][:, i : i + 1], accum_out=spread[:, i : i + 1],
                 )
             nc.scalar.activation(
-                out=rstds[pair][:], in_=spread[:], func=ACT.Abs_reciprocal_sqrt,
+                out=rstds[blk][:], in_=spread[:], func=ACT.Abs_reciprocal_sqrt,
                 scale=1.0 / DIM, bias=eps[:],
             )
 
-        def normalise(pair):
-            x_pair = pair_rows(pair)
-            xhats[pair] = work.tile([P, PAIR, PACK, P], F32, name="xhat")
-            for i in range(PAIR):
+        def statistics_on_vector(blk):
+            moments = small.tile([P, TILES, 6], F32, name="moments")
+            mean_var = small.tile([P, TILES, 2], F32, name="mean_var")
+            neg_means[blk] = small.tile([P, TILES], F32, name="neg_mean")
+            rstds[blk] = small.tile([P, TILES], F32, name="rstd")
+            for i in range(TILES):
+                nc.vector.bn_stats(out=moments[:, i, :], in_=x_blocks[blk][:, i, :])
+                nc.vector.bn_aggr(out=mean_var[:, i, :], in_=moments[:, i, :])
+            nc.vector.tensor_scalar_mul(out=neg_means[blk][:], in0=mean_var[:, :, 0], scalar1=-1.0)
+            nc.scalar.activation(
+                out=rstds[blk][:], in_=mean_var[:, :, 1], func=ACT.Abs_reciprocal_sqrt, bias=eps[:]
+            )
+
+        def normalise(blk):
+            xhats[blk] = work.tile([P, TILES, PACK, P], F32, name="xhat")
+            for i in range(TILES):
                 nc.gpsimd.tensor_scalar(
-                    out=xhats[pair][:, i, :, :],
-                    in0=x_pair[:, i, :].rearrange("n (p t) -> n t p", t=PACK),
-                    scalar1=neg_means[pair][:, i : i + 1], scalar2=rstds[pair][:, i : i + 1],
+                    out=xhats[blk][:, i, :, :],
+                    in0=x_blocks[blk][:, i, :].rearrange("n (p t) -> n t p", t=PACK),
+                    scalar1=neg_means[blk][:, i : i + 1], scalar2=rstds[blk][:, i : i + 1],
                     op0=ALU.add, op1=ALU.mult,
                 )
 
-        def transpose(pair):
-            banks[pair] = [
-                psum_t.tile([P, PACK // 2, PAIR_TOKENS], F32, name="xhat_t%d" % u) for u in range(2)
-            ]
-            for i in range(PAIR):
+        def transpose(blk):
+            banks[blk] = [psum_t.tile([P, BLOCK], F32, name="xhat_t%d" % t) for t in range(PACK)]
+            for i in range(TILES):
                 for t in range(PACK):
                     nc.tensor.transpose(
-                        out=banks[pair][t // 2][:, t % 2, i * P : (i + 1) * P],
-                        in_=xhats[pair][:, i, t, :], identity=ident[:],
+                        out=banks[blk][t][:, i * P : (i + 1) * P], in_=xhats[blk][:, i, t, :],
+                        identity=ident[:],
                     )
 
-        def modulate(pair):
-            b = pair // (PAIRS_PER_BLOCK * BLOCKS_PER_BATCH)
-            planes[pair] = work.tile([P, PACK, PAIR_TOKENS], BF16, name="planes")
+        def modulate(blk):
+            b = blk // BLOCKS_PER_BATCH
+            planes[blk] = work.tile([P, PACK, BLOCK], BF16, name="planes")
             for t in range(PACK):
                 nc.scalar.activation(
-                    out=planes[pair][:, t, :], in_=banks[pair][t // 2][:, t % 2, :], func=ACT.Identity,
+                    out=planes[blk][:, t, :], in_=banks[blk][t][:], func=ACT.Identity,
                     scale=mod_gain[:, b, t : t + 1], bias=mod_shift[:, b, t : t + 1],
                 )
 
-        def regroup(pair):
-            grouped[pair] = work.tile([P, PAIR_TOKENS, PACK], BF16, name="grouped", align_bytes=64)
+        def regroup(blk):
+            grouped[blk] = work.tile([P, BLOCK, PACK], BF16, name="grouped", align_bytes=64)
             nc.gpsimd.tensor_scalar(
-                out=grouped[pair][:], in0=planes[pair][:].rearrange("p t n -> p n t"),
+                out=grouped[blk][:], in0=planes[blk][:].rearrange("p t n -> p n t"),
                 scalar1=1.0, scalar2=0.0, op0=ALU.mult, op1=ALU.add,
             )
 
-        def quantise(pair):
-            words[pair] = packed.tile([P, PAIR_TOKENS], U32, name="words", align_bytes=64)
-            scales[pair] = packed.tile([P, PAIR_TOKENS], U8, name="scales", align_bytes=64)
+        def quantise(blk):
+            words[blk] = work.tile([P, BLOCK], U32, name="words", align_bytes=64)
+            scales[blk] = work.tile([P, BLOCK], U8, name="scales", align_bytes=64)
             nc.vector.quantize_mx(
-                out=words[pair][:].bitcast(FP8X4), scales=scales[pair][:],
-                in_=grouped[pair][:].rearrange("p n t -> p (n t)"),
+                out=words[blk][:].bitcast(FP8X4), scales=scales[blk][:],
+                in_=grouped[blk][:].rearrange("p n t -> p (n t)"),
             )
 
         def project(blk, j):
@@ -191,12 +195,11 @@ def tile_localattentionblock_pa_t_kernel(
             cols = slice(j * PROJ_COLS, (j + 1) * PROJ_COLS)
             result = results.tile([P, HEADS, TILES, HEAD_DIM], F32, name="result")
             for i in range(TILES):
-                pair = blk * PAIRS_PER_BLOCK + i // PAIR
-                tokens = slice((i % PAIR) * P, (i % PAIR + 1) * P)
+                tokens = slice(i * P, (i + 1) * P)
                 acc = psum_acc.tile([P, PROJ_COLS], F32, name="acc")
                 nc.tensor.matmul_mx(
                     out=acc[:],
-                    lhsT=words[pair][:, tokens].bitcast(FP8X4), lhsT_scale=scales[pair][:, tokens],
+                    lhsT=words[blk][:, tokens].bitcast(FP8X4), lhsT_scale=scales[blk][:, tokens],
                     rhs=w_words[:, cols].bitcast(FP8X4), rhs_scale=w_scales[:, cols],
                     start=True, stop=True,
                 )
@@ -213,38 +216,32 @@ def tile_localattentionblock_pa_t_kernel(
                 in_=result[:],
             )
 
-        def when_there(stage, pair):
-            if pair < N_PAIRS:
-                stage(pair)
-
-        def norm_step(pair):
-            when_there(statistics, pair + 2)
-            when_there(modulate, pair + 1)
-            when_there(normalise, pair + 2)
-            when_there(regroup, pair + 1)
-
-        statistics(0)
+        statistics_on_vector(0)
         normalise(0)
         transpose(0)
-        statistics(1)
+        statistics_on_vector(1)
         normalise(1)
+        statistics_on_vector(2)
+        fold_modulation()
+        quantise_weights()
         modulate(0)
         regroup(0)
-        quantise_weights()
         quantise(0)
         transpose(1)
-        norm_step(0)
-        quantise(1)
-        transpose(2)
 
         for blk in range(N_BLOCKS):
-            first = blk * PAIRS_PER_BLOCK
-            norm_step(first + 1)
+            if blk + HEAD_BLOCKS < N_BLOCKS:
+                statistics(blk + HEAD_BLOCKS)
+            if blk + 1 < N_BLOCKS:
+                modulate(blk + 1)
+            if blk + 2 < N_BLOCKS:
+                normalise(blk + 2)
+            if blk + 1 < N_BLOCKS:
+                regroup(blk + 1)
             project(blk, 0)
-            when_there(transpose, first + 3)
-            norm_step(first + 2)
             project(blk, 1)
-            when_there(quantise, first + 2)
+            if blk + 2 < N_BLOCKS:
+                transpose(blk + 2)
+            if blk + 1 < N_BLOCKS:
+                quantise(blk + 1)
             project(blk, 2)
-            when_there(transpose, first + 4)
-            when_there(quantise, first + 3)

@@ -17,12 +17,16 @@ BATCH, TOKENS, DIM = 4, 1024, 512
 PROJ, HEADS, HEAD_DIM = 3, 4, 128
 PROJ_COLS = HEADS * HEAD_DIM
 OUT_COLS = PROJ * PROJ_COLS
-TILES = 4
-BLOCK = TILES * P
-BLOCKS_PER_BATCH = TOKENS // BLOCK
-N_BLOCKS = BATCH * BLOCKS_PER_BATCH
-HEAD_BLOCKS = 3
+QUARTERS = DIM // P
 EPS = 1e-5
+
+SPANS = ((2, 2, 4), (4, 4), (4, 4), (4, 2, 2))
+CHAIN = 2
+FOLD_SLOTS = 4
+
+AHEAD_STATISTICS = 3
+AHEAD_MODULATE = 2
+AHEAD_QUANTISE = 1
 
 assert DIM == P * PACK
 
@@ -33,48 +37,78 @@ def tile_localattentionblock_pa_t_kernel(
     tc, x, t_scale, t_shift, ln1_g, ln1_b, qkv_w, qkv_b, out
 ):
     nc = tc.nc
+    regions = []
+    chains = []
+    for b in range(BATCH):
+        first_token = 0
+        for span in SPANS[b]:
+            regions.append((b, first_token, span))
+            for i0 in range(0, span, CHAIN):
+                chains.append((b, len(regions) - 1, i0, min(CHAIN, span)))
+            first_token += span * P
+    n_chains = len(chains)
+
     with ExitStack() as ctx:
         const = ctx.enter_context(tc.tile_pool(name="const", bufs=1))
         rows = ctx.enter_context(tc.tile_pool(name="rows", bufs=1))
-        small = ctx.enter_context(tc.tile_pool(name="small", bufs=4))
+        small = ctx.enter_context(tc.tile_pool(name="small", bufs=6))
         work = ctx.enter_context(tc.tile_pool(name="work", bufs=2))
-        results = ctx.enter_context(tc.tile_pool(name="results", bufs=6))
-        psum_t = ctx.enter_context(tc.psum_pool(name="psum_t", bufs=1))
-        psum_acc = ctx.enter_context(tc.psum_pool(name="psum_acc", bufs=4))
+        results = ctx.enter_context(tc.tile_pool(name="results", bufs=2))
+        psum_t = ctx.enter_context(tc.psum_pool(name="psum_t", bufs=2))
+        psum_f = ctx.enter_context(tc.psum_pool(name="psum_f", bufs=1))
+        psum_acc = ctx.enter_context(tc.psum_pool(name="psum_acc", bufs=3))
         ctx.enter_context(tc.manual_schedule())
 
-        def load_block(blk):
-            b, half = divmod(blk, BLOCKS_PER_BATCH)
-            x_blk = rows.tile([P, TILES, DIM], BF16, name="x_blk%d" % blk)
+        x_regions = []
+
+        def load_region():
+            b, first_token, span = regions[len(x_regions)]
+            x_reg = rows.tile([P, span, DIM], BF16, name="x_reg%d" % len(x_regions))
             nc.sync.dma_start(
-                out=x_blk[:],
-                in_=x[b, half * BLOCK : (half + 1) * BLOCK, :].rearrange(
-                    "(p i) k -> p i k", i=TILES
+                out=x_reg[:],
+                in_=x[b, first_token : first_token + span * P, :].rearrange(
+                    "(p i) k -> p i k", i=span
                 ),
             )
-            return x_blk
+            x_regions.append(x_reg)
 
-        x_blocks = [load_block(blk) for blk in range(HEAD_BLOCKS)]
         w_rows = const.tile([P, PACK, OUT_COLS], BF16)
-        nc.sync.dma_start(out=w_rows[:], in_=qkv_w.rearrange("(p t) c -> p t c", t=PACK))
-        for blk in range(HEAD_BLOCKS, N_BLOCKS):
-            x_blocks.append(load_block(blk))
+
+        def load_weights(j):
+            cols = slice(j * PROJ_COLS, (j + 1) * PROJ_COLS)
+            nc.sync.dma_start(
+                out=w_rows[:, :, cols],
+                in_=qkv_w.rearrange("(p t) c -> p t c", t=PACK)[:, :, cols],
+            )
 
         ln_gain = const.tile([P, PACK], BF16)
         ln_shift = const.tile([P, PACK], BF16)
         time_scale = const.tile([P, BATCH, PACK], BF16)
         time_shift = const.tile([P, BATCH, PACK], BF16)
+        bias_rows = const.tile([P, OUT_COLS], BF16)
+
+        load_region()
+        load_region()
         nc.scalar.dma_start(out=ln_gain[:], in_=ln1_g.rearrange("(p t) -> p t", t=PACK))
         nc.scalar.dma_start(out=ln_shift[:], in_=ln1_b.rearrange("(p t) -> p t", t=PACK))
-        nc.scalar.dma_start(out=time_scale[:], in_=t_scale.rearrange("b (p t) -> p b t", t=PACK))
-        nc.scalar.dma_start(out=time_shift[:], in_=t_shift.rearrange("b (p t) -> p b t", t=PACK))
-        bias_rows = const.tile([P, OUT_COLS], BF16)
-        nc.scalar.dma_start(out=bias_rows[:], in_=qkv_b.partition_broadcast(P))
+        nc.sync.dma_start(out=time_scale[:], in_=t_scale.rearrange("b (p t) -> p b t", t=PACK))
+        nc.sync.dma_start(out=time_shift[:], in_=t_shift.rearrange("b (p t) -> p b t", t=PACK))
+        load_weights(0)
+        load_region()
+        load_weights(1)
+        load_weights(2)
+        nc.sync.dma_start(out=bias_rows[:], in_=qkv_b.partition_broadcast(P))
+        for r in range(len(x_regions), len(regions)):
+            load_region()
 
-        ident = const.tile([P, P], F32)
-        make_identity(nc, ident[:])
         eps = const.tile([P, 1], F32)
         nc.vector.memset(eps[:], EPS)
+        warm = const.tile([P, 1], F32)
+        nc.scalar.activation(out=warm[:], in_=eps[:], func=ACT.Abs_reciprocal_sqrt)
+        ident = const.tile([P, P], F32)
+        make_identity(nc, ident[:])
+        ident_bf = const.tile([P, P], BF16)
+        make_identity(nc, ident_bf[:])
 
         one_plus = const.tile([P, BATCH, PACK], F32)
         mod_gain = const.tile([P, BATCH, PACK], F32)
@@ -95,153 +129,181 @@ def tile_localattentionblock_pa_t_kernel(
         w_words = const.tile([P, OUT_COLS], U32, align_bytes=64)
         w_scales = const.tile([P, OUT_COLS], U8, align_bytes=64)
 
-        def quantise_weights():
-            for j in range(PROJ):
-                cols = slice(j * PROJ_COLS, (j + 1) * PROJ_COLS)
-                nc.vector.tensor_copy(
-                    out=w_grouped[:, cols, :], in_=w_rows[:, :, cols].rearrange("p t c -> p c t")
-                )
-            for j in range(PROJ):
-                cols = slice(j * PROJ_COLS, (j + 1) * PROJ_COLS)
-                nc.vector.quantize_mx(
-                    out=w_words[:, cols].bitcast(FP8X4),
-                    scales=w_scales[:, cols],
-                    in_=w_grouped[:, cols, :].rearrange("p c t -> p (c t)"),
+        def quantise_weights(j):
+            cols = slice(j * PROJ_COLS, (j + 1) * PROJ_COLS)
+            nc.vector.tensor_copy(
+                out=w_grouped[:, cols, :], in_=w_rows[:, :, cols].rearrange("p t c -> p c t")
+            )
+            nc.vector.quantize_mx(
+                out=w_words[:, cols].bitcast(FP8X4),
+                scales=w_scales[:, cols],
+                in_=w_grouped[:, cols, :].rearrange("p c t -> p (c t)"),
+            )
+
+        slots, neg_means, rstds, xhats, planes_t, planes, grouped, words, scales = (
+            {}, {}, {}, {}, {}, {}, {}, {}, {},
+        )
+        folded = psum_f.tile([P, FOLD_SLOTS, P], F32, name="folded")
+        folds_done = [0]
+
+        def fold(c):
+            if c == 0:
+                return
+            b, r, i0, tiles = chains[c]
+            slots[c] = folds_done[0] % FOLD_SLOTS
+            folds_done[0] += CHAIN
+            for u in range(QUARTERS):
+                nc.tensor.matmul(
+                    out=folded[:, slots[c] : slots[c] + tiles, :], lhsT=ident_bf[:],
+                    rhs=x_regions[r][:, i0 : i0 + tiles, u * P : (u + 1) * P],
+                    start=(u == 0), stop=(u == QUARTERS - 1),
                 )
 
-        neg_means, rstds, xhats, banks, planes, grouped, words, scales = {}, {}, {}, {}, {}, {}, {}, {}
-
-        def statistics(blk):
-            x_blk = x_blocks[blk]
-            unread = work.tile([P, TILES, DIM], BF16, name="unread")
-            total = small.tile([P, TILES], F32, name="total")
-            spread = small.tile([P, TILES], F32, name="spread")
-            neg_means[blk] = small.tile([P, TILES], F32, name="neg_mean")
-            rstds[blk] = small.tile([P, TILES], F32, name="rstd")
-            for i in range(TILES):
-                nc.scalar.activation(
-                    out=unread[:, i, :], in_=x_blk[:, i, :], func=ACT.Identity,
-                    accum_out=total[:, i : i + 1],
+        def statistics(c):
+            b, r, i0, tiles = chains[c]
+            rstds[c] = small.tile([P, CHAIN], F32, name="rstd")
+            if c == 0:
+                moments = small.tile([P, CHAIN, 6], F32, name="moments")
+                mean_var = small.tile([P, CHAIN, 2], F32, name="mean_var")
+                for i in range(tiles):
+                    nc.vector.bn_stats(out=moments[:, i, :], in_=x_regions[r][:, i0 + i, :])
+                    nc.vector.bn_aggr(out=mean_var[:, i, :], in_=moments[:, i, :])
+                neg_means[c] = small.tile([P, CHAIN], F32, name="neg_mean")
+                nc.vector.tensor_scalar_mul(
+                    out=neg_means[c][:, :tiles], in0=mean_var[:, :tiles, 0], scalar1=-1.0
                 )
-            nc.scalar.mul(out=neg_means[blk][:], in_=total[:], mul=-1.0 / DIM)
-            for i in range(TILES):
                 nc.scalar.activation(
-                    out=unread[:, i, :], in_=x_blk[:, i, :], func=ACT.Square,
-                    bias=neg_means[blk][:, i : i + 1], accum_out=spread[:, i : i + 1],
+                    out=rstds[c][:, :tiles], in_=mean_var[:, :tiles, 1],
+                    func=ACT.Abs_reciprocal_sqrt, bias=eps[:],
+                )
+                return
+            unread = work.tile([P, CHAIN, DIM], BF16, name="unread")
+            neg_mean = small.tile([P, CHAIN], F32, name="neg_mean")
+            spread = small.tile([P, CHAIN], F32, name="spread")
+            neg_means[c] = neg_mean
+            for i in range(tiles):
+                nc.scalar.activation(
+                    out=unread[:, i, :P], in_=folded[:, slots[c] + i, :], func=ACT.Identity,
+                    scale=-1.0 / DIM, accum_out=neg_mean[:, i : i + 1],
+                )
+            for i in range(tiles):
+                nc.scalar.activation(
+                    out=unread[:, i, :], in_=x_regions[r][:, i0 + i, :], func=ACT.Square,
+                    bias=neg_mean[:, i : i + 1], accum_out=spread[:, i : i + 1],
                 )
             nc.scalar.activation(
-                out=rstds[blk][:], in_=spread[:], func=ACT.Abs_reciprocal_sqrt,
+                out=rstds[c][:, :tiles], in_=spread[:, :tiles], func=ACT.Abs_reciprocal_sqrt,
                 scale=1.0 / DIM, bias=eps[:],
             )
 
-        def statistics_on_vector(blk):
-            moments = small.tile([P, TILES, 6], F32, name="moments")
-            mean_var = small.tile([P, TILES, 2], F32, name="mean_var")
-            neg_means[blk] = small.tile([P, TILES], F32, name="neg_mean")
-            rstds[blk] = small.tile([P, TILES], F32, name="rstd")
-            for i in range(TILES):
-                nc.vector.bn_stats(out=moments[:, i, :], in_=x_blocks[blk][:, i, :])
-                nc.vector.bn_aggr(out=mean_var[:, i, :], in_=moments[:, i, :])
-            nc.vector.tensor_scalar_mul(out=neg_means[blk][:], in0=mean_var[:, :, 0], scalar1=-1.0)
-            nc.scalar.activation(
-                out=rstds[blk][:], in_=mean_var[:, :, 1], func=ACT.Abs_reciprocal_sqrt, bias=eps[:]
-            )
-
-        def normalise(blk):
-            xhats[blk] = work.tile([P, TILES, PACK, P], F32, name="xhat")
-            for i in range(TILES):
-                nc.gpsimd.tensor_scalar(
-                    out=xhats[blk][:, i, :, :],
-                    in0=x_blocks[blk][:, i, :].rearrange("n (p t) -> n t p", t=PACK),
-                    scalar1=neg_means[blk][:, i : i + 1], scalar2=rstds[blk][:, i : i + 1],
+        def normalise(c):
+            b, r, i0, tiles = chains[c]
+            xhats[c] = work.tile([P, CHAIN, PACK, P], F32, name="xhat")
+            engine = nc.vector if c == 0 else nc.gpsimd
+            for i in range(tiles):
+                engine.tensor_scalar(
+                    out=xhats[c][:, i, :, :],
+                    in0=x_regions[r][:, i0 + i, :].rearrange("n (p t) -> n t p", t=PACK),
+                    scalar1=neg_means[c][:, i : i + 1], scalar2=rstds[c][:, i : i + 1],
                     op0=ALU.add, op1=ALU.mult,
                 )
 
-        def transpose(blk):
-            banks[blk] = [psum_t.tile([P, BLOCK], F32, name="xhat_t%d" % t) for t in range(PACK)]
-            for i in range(TILES):
+        def transpose(c):
+            tiles = chains[c][3]
+            pair = [psum_t.tile([P, 2, CHAIN * P], F32, name="xhat_t%d" % u) for u in range(2)]
+            planes_t[c] = [pair[t // 2][:, t % 2, :] for t in range(PACK)]
+            for i in range(tiles):
                 for t in range(PACK):
                     nc.tensor.transpose(
-                        out=banks[blk][t][:, i * P : (i + 1) * P], in_=xhats[blk][:, i, t, :],
+                        out=planes_t[c][t][:, i * P : (i + 1) * P], in_=xhats[c][:, i, t, :],
                         identity=ident[:],
                     )
 
-        def modulate(blk):
-            b = blk // BLOCKS_PER_BATCH
-            planes[blk] = work.tile([P, PACK, BLOCK], BF16, name="planes")
+        def modulate(c):
+            b, r, i0, tiles = chains[c]
+            planes[c] = work.tile([P, PACK, CHAIN * P], BF16, name="planes")
             for t in range(PACK):
                 nc.scalar.activation(
-                    out=planes[blk][:, t, :], in_=banks[blk][t][:], func=ACT.Identity,
+                    out=planes[c][:, t, : tiles * P], in_=planes_t[c][t][:, : tiles * P],
+                    func=ACT.Identity,
                     scale=mod_gain[:, b, t : t + 1], bias=mod_shift[:, b, t : t + 1],
                 )
 
-        def regroup(blk):
-            grouped[blk] = work.tile([P, BLOCK, PACK], BF16, name="grouped", align_bytes=64)
-            nc.gpsimd.tensor_scalar(
-                out=grouped[blk][:], in0=planes[blk][:].rearrange("p t n -> p n t"),
-                scalar1=1.0, scalar2=0.0, op0=ALU.mult, op1=ALU.add,
-            )
+        def regroup(c):
+            tiles = chains[c][3]
+            grouped[c] = work.tile([P, CHAIN * P, PACK], BF16, name="grouped", align_bytes=64)
+            woven = planes[c][:, :, : tiles * P].rearrange("p t n -> p n t")
+            if c == 0:
+                nc.vector.tensor_copy(out=grouped[c][:, : tiles * P, :], in_=woven)
+            else:
+                nc.gpsimd.tensor_scalar(
+                    out=grouped[c][:, : tiles * P, :], in0=woven,
+                    scalar1=1.0, scalar2=0.0, op0=ALU.mult, op1=ALU.add,
+                )
 
-        def quantise(blk):
-            words[blk] = work.tile([P, BLOCK], U32, name="words", align_bytes=64)
-            scales[blk] = work.tile([P, BLOCK], U8, name="scales", align_bytes=64)
+        def quantise(c):
+            tiles = chains[c][3]
+            words[c] = work.tile([P, CHAIN * P], U32, name="words", align_bytes=64)
+            scales[c] = work.tile([P, CHAIN * P], U8, name="scales", align_bytes=64)
             nc.vector.quantize_mx(
-                out=words[blk][:].bitcast(FP8X4), scales=scales[blk][:],
-                in_=grouped[blk][:].rearrange("p n t -> p (n t)"),
+                out=words[c][:, : tiles * P].bitcast(FP8X4), scales=scales[c][:, : tiles * P],
+                in_=grouped[c][:, : tiles * P, :].rearrange("p n t -> p (n t)"),
             )
 
-        def project(blk, j):
-            b, half = divmod(blk, BLOCKS_PER_BATCH)
+        open_results = {}
+
+        def project(c, j):
+            b, r, i0, tiles = chains[c]
+            first_token, span = regions[r][1], regions[r][2]
             cols = slice(j * PROJ_COLS, (j + 1) * PROJ_COLS)
-            result = results.tile([P, HEADS, TILES, HEAD_DIM], F32, name="result")
-            for i in range(TILES):
+            if i0 == 0:
+                open_results[j] = results.tile([P, HEADS, span, HEAD_DIM], F32, name="result%d" % j)
+            result = open_results[j]
+            for i in range(tiles):
                 tokens = slice(i * P, (i + 1) * P)
                 acc = psum_acc.tile([P, PROJ_COLS], F32, name="acc")
                 nc.tensor.matmul_mx(
                     out=acc[:],
-                    lhsT=words[blk][:, tokens].bitcast(FP8X4), lhsT_scale=scales[blk][:, tokens],
+                    lhsT=words[c][:, tokens].bitcast(FP8X4), lhsT_scale=scales[c][:, tokens],
                     rhs=w_words[:, cols].bitcast(FP8X4), rhs_scale=w_scales[:, cols],
                     start=True, stop=True,
                 )
                 nc.vector.tensor_tensor(
-                    out=result[:, :, i, :],
+                    out=result[:, :, i0 + i, :],
                     in0=acc[:].rearrange("p (h d) -> p h d", h=HEADS),
                     in1=bias_rows[:, cols].rearrange("p (h d) -> p h d", h=HEADS),
                     op=ALU.add,
                 )
-            nc.sync.dma_start(
-                out=out[j, b, :, half * BLOCK : (half + 1) * BLOCK, :].rearrange(
-                    "h (p i) d -> p h i d", i=TILES
-                ),
-                in_=result[:],
-            )
+            if i0 + tiles == span:
+                nc.sync.dma_start(
+                    out=out[j, b, :, first_token : first_token + span * P, :].rearrange(
+                        "h (p i) d -> p h i d", i=span
+                    ),
+                    in_=result[:],
+                )
 
-        statistics_on_vector(0)
-        normalise(0)
-        transpose(0)
-        statistics_on_vector(1)
-        normalise(1)
-        statistics_on_vector(2)
-        fold_modulation()
-        quantise_weights()
-        modulate(0)
-        regroup(0)
-        quantise(0)
-        transpose(1)
+        def run(stage, c):
+            if 0 <= c < n_chains:
+                stage(c)
 
-        for blk in range(N_BLOCKS):
-            if blk + HEAD_BLOCKS < N_BLOCKS:
-                statistics(blk + HEAD_BLOCKS)
-            if blk + 1 < N_BLOCKS:
-                modulate(blk + 1)
-            if blk + 2 < N_BLOCKS:
-                normalise(blk + 2)
-            if blk + 1 < N_BLOCKS:
-                regroup(blk + 1)
-            project(blk, 0)
-            project(blk, 1)
-            if blk + 2 < N_BLOCKS:
-                transpose(blk + 2)
-            if blk + 1 < N_BLOCKS:
-                quantise(blk + 1)
-            project(blk, 2)
+        for s in range(-AHEAD_STATISTICS, n_chains):
+            if s >= 0:
+                project(s, 0)
+            run(fold, s + AHEAD_STATISTICS)
+            run(statistics, s + AHEAD_STATISTICS)
+            if s == -AHEAD_STATISTICS:
+                fold_modulation()
+            run(regroup, s + AHEAD_QUANTISE)
+            if s >= 0:
+                project(s, 1)
+            run(quantise, s + AHEAD_QUANTISE)
+            if s == -1:
+                quantise_weights(1)
+                quantise_weights(2)
+            if s >= 0:
+                project(s, 2)
+            run(normalise, s + AHEAD_STATISTICS)
+            if s == -AHEAD_MODULATE:
+                quantise_weights(0)
+            run(transpose, s + AHEAD_MODULATE)
+            run(modulate, s + AHEAD_MODULATE)

@@ -251,6 +251,7 @@ def tile_localattentionblock_pa_t_kernel(
             )
 
         open_results = {}
+        waiting_stores = []
 
         def project(c, j):
             b, r, i0, tiles = chains[c]
@@ -275,12 +276,13 @@ def tile_localattentionblock_pa_t_kernel(
                     op=ALU.add,
                 )
             if i0 + tiles == span:
-                nc.sync.dma_start(
-                    out=out[j, b, :, first_token : first_token + span * P, :].rearrange(
-                        "h (p i) d -> p h i d", i=span
-                    ),
-                    in_=result[:],
+                target = out[j, b, :, first_token : first_token + span * P, :].rearrange(
+                    "h (p i) d -> p h i d", i=span
                 )
+                if j == 1 and c < n_chains - 1:
+                    waiting_stores.append((target, result))
+                else:
+                    nc.sync.dma_start(out=target, in_=result[:])
 
         def run(stage, c):
             if 0 <= c < n_chains:
@@ -307,3 +309,6 @@ def tile_localattentionblock_pa_t_kernel(
                 quantise_weights(0)
             run(transpose, s + AHEAD_MODULATE)
             run(modulate, s + AHEAD_MODULATE)
+            for target, result in waiting_stores:
+                nc.scalar.dma_start(out=target, in_=result[:])
+            waiting_stores.clear()

@@ -51,9 +51,9 @@ def tile_localattentionblock_pa_t_kernel(
     with ExitStack() as ctx:
         const = ctx.enter_context(tc.tile_pool(name="const", bufs=1))
         rows = ctx.enter_context(tc.tile_pool(name="rows", bufs=1))
-        small = ctx.enter_context(tc.tile_pool(name="small", bufs=6))
-        work = ctx.enter_context(tc.tile_pool(name="work", bufs=2))
-        results = ctx.enter_context(tc.tile_pool(name="results", bufs=2))
+        small = ctx.enter_context(tc.tile_pool(name="small", bufs=8))
+        work = ctx.enter_context(tc.tile_pool(name="work", bufs=4))
+        results = ctx.enter_context(tc.tile_pool(name="results", bufs=3))
         psum_t = ctx.enter_context(tc.psum_pool(name="psum_t", bufs=2))
         psum_f = ctx.enter_context(tc.psum_pool(name="psum_f", bufs=1))
         psum_acc = ctx.enter_context(tc.psum_pool(name="psum_acc", bufs=3))
@@ -212,12 +212,13 @@ def tile_localattentionblock_pa_t_kernel(
             tiles = chains[c][3]
             pair = [psum_t.tile([P, 2, CHAIN * P], F32, name="xhat_t%d" % u) for u in range(2)]
             planes_t[c] = [pair[t // 2][:, t % 2, :] for t in range(PACK)]
-            for i in range(tiles):
-                for t in range(PACK):
-                    nc.tensor.transpose(
-                        out=planes_t[c][t][:, i * P : (i + 1) * P], in_=xhats[c][:, i, t, :],
-                        identity=ident[:],
-                    )
+            for u in range(2):
+                for i in range(tiles):
+                    for t in (2 * u, 2 * u + 1):
+                        nc.tensor.transpose(
+                            out=planes_t[c][t][:, i * P : (i + 1) * P], in_=xhats[c][:, i, t, :],
+                            identity=ident[:],
+                        )
 
         def modulate(c):
             b, r, i0, tiles = chains[c]

@@ -22,7 +22,6 @@ EPS = 1e-5
 
 SPANS = ((2, 2, 4), (4, 4), (4, 4), (4, 2, 2))
 CHAIN = 2
-FOLD_SLOTS = 4
 
 AHEAD_STATISTICS = 3
 AHEAD_MODULATE = 2
@@ -55,8 +54,7 @@ def tile_localattentionblock_pa_t_kernel(
         work = ctx.enter_context(tc.tile_pool(name="work", bufs=4))
         results = ctx.enter_context(tc.tile_pool(name="results", bufs=3))
         psum_t = ctx.enter_context(tc.psum_pool(name="psum_t", bufs=2))
-        psum_f = ctx.enter_context(tc.psum_pool(name="psum_f", bufs=1))
-        psum_acc = ctx.enter_context(tc.psum_pool(name="psum_acc", bufs=3))
+        psum_acc = ctx.enter_context(tc.psum_pool(name="psum_acc", bufs=4))
         ctx.enter_context(tc.manual_schedule())
 
         x_regions = []
@@ -140,21 +138,19 @@ def tile_localattentionblock_pa_t_kernel(
                 in_=w_grouped[:, cols, :].rearrange("p c t -> p (c t)"),
             )
 
-        slots, neg_means, rstds, xhats, planes_t, planes, grouped, words, scales = (
-            {}, {}, {}, {}, {}, {}, {}, {}, {},
+        neg_means, rstds, xhats, planes_t, planes, grouped, words, scales = (
+            {}, {}, {}, {}, {}, {}, {}, {},
         )
-        folded = psum_f.tile([P, FOLD_SLOTS, P], F32, name="folded")
-        folds_done = [0]
+        folds = {}
 
         def fold(c):
             if c == 0:
                 return
             b, r, i0, tiles = chains[c]
-            slots[c] = folds_done[0] % FOLD_SLOTS
-            folds_done[0] += CHAIN
+            folds[c] = psum_acc.tile([P, PROJ_COLS // P, P], F32, name="acc")
             for u in range(QUARTERS):
                 nc.tensor.matmul(
-                    out=folded[:, slots[c] : slots[c] + tiles, :], lhsT=ident_bf[:],
+                    out=folds[c][:, :tiles, :], lhsT=ident_bf[:],
                     rhs=x_regions[r][:, i0 : i0 + tiles, u * P : (u + 1) * P],
                     start=(u == 0), stop=(u == QUARTERS - 1),
                 )
@@ -183,7 +179,7 @@ def tile_localattentionblock_pa_t_kernel(
             neg_means[c] = neg_mean
             for i in range(tiles):
                 nc.scalar.activation(
-                    out=unread[:, i, :P], in_=folded[:, slots[c] + i, :], func=ACT.Identity,
+                    out=unread[:, i, :P], in_=folds[c][:, i, :], func=ACT.Identity,
                     scale=-1.0 / DIM, accum_out=neg_mean[:, i : i + 1],
                 )
             for i in range(tiles):

@@ -127,11 +127,16 @@ def tile_localattentionblock_pa_t_kernel(
         w_words = const.tile([P, OUT_COLS], U32, align_bytes=64)
         w_scales = const.tile([P, OUT_COLS], U8, align_bytes=64)
 
+        def regroup_weights(j):
+            cols = slice(j * PROJ_COLS, (j + 1) * PROJ_COLS)
+            woven = w_rows[:, :, cols].rearrange("p t c -> p c t")
+            if j == PROJ - 1:
+                nc.scalar.copy(out=w_grouped[:, cols, :], in_=woven)
+            else:
+                nc.vector.tensor_copy(out=w_grouped[:, cols, :], in_=woven)
+
         def quantise_weights(j):
             cols = slice(j * PROJ_COLS, (j + 1) * PROJ_COLS)
-            nc.vector.tensor_copy(
-                out=w_grouped[:, cols, :], in_=w_rows[:, :, cols].rearrange("p t c -> p c t")
-            )
             nc.vector.quantize_mx(
                 out=w_words[:, cols].bitcast(FP8X4),
                 scales=w_scales[:, cols],
@@ -297,13 +302,16 @@ def tile_localattentionblock_pa_t_kernel(
                 project(s, 1)
             run(quantise, s + AHEAD_QUANTISE)
             if s == -1:
+                regroup_weights(2)
                 quantise_weights(1)
                 quantise_weights(2)
             if s >= 0:
                 project(s, 2)
             run(normalise, s + AHEAD_STATISTICS)
             if s == -AHEAD_MODULATE:
+                regroup_weights(0)
                 quantise_weights(0)
+                regroup_weights(1)
             run(transpose, s + AHEAD_MODULATE)
             run(modulate, s + AHEAD_MODULATE)
             for target, result in waiting_stores:

@@ -53,8 +53,8 @@ def tile_localattentionblock_pa_t_kernel(
         small = ctx.enter_context(tc.tile_pool(name="small", bufs=8))
         work = ctx.enter_context(tc.tile_pool(name="work", bufs=4))
         results = ctx.enter_context(tc.tile_pool(name="results", bufs=3))
-        psum_t = ctx.enter_context(tc.psum_pool(name="psum_t", bufs=2))
-        psum_acc = ctx.enter_context(tc.psum_pool(name="psum_acc", bufs=4))
+        psum_t = ctx.enter_context(tc.psum_pool(name="psum_t", bufs=1))
+        psum_acc = ctx.enter_context(tc.psum_pool(name="psum_acc", bufs=6))
         ctx.enter_context(tc.manual_schedule())
 
         x_regions = []

@@ -20,7 +20,7 @@ OUT_COLS = PROJ * PROJ_COLS
 QUARTERS = DIM // P
 EPS = 1e-5
 
-SPANS = ((2, 2, 4), (4, 4), (4, 4), (4, 2, 2))
+SPANS = ((2, 2, 2, 2), (2, 2, 4), (4, 4), (4, 4))
 CHAIN = 2
 
 AHEAD_STATISTICS = 3
@@ -293,6 +293,8 @@ def tile_localattentionblock_pa_t_kernel(
         for s in range(-AHEAD_STATISTICS, n_chains):
             if s >= 0:
                 project(s, 0)
+            if s == 0:
+                quantise_weights(2)
             run(fold, s + AHEAD_STATISTICS)
             run(statistics, s + AHEAD_STATISTICS)
             if s == -AHEAD_STATISTICS:
@@ -302,18 +304,20 @@ def tile_localattentionblock_pa_t_kernel(
                 project(s, 1)
             run(quantise, s + AHEAD_QUANTISE)
             if s == -1:
+                regroup_weights(1)
                 regroup_weights(2)
                 quantise_weights(1)
-                quantise_weights(2)
             if s >= 0:
+                run(transpose, s + AHEAD_MODULATE)
+                run(modulate, s + AHEAD_MODULATE)
                 project(s, 2)
             run(normalise, s + AHEAD_STATISTICS)
             if s == -AHEAD_MODULATE:
                 regroup_weights(0)
                 quantise_weights(0)
-                regroup_weights(1)
-            run(transpose, s + AHEAD_MODULATE)
-            run(modulate, s + AHEAD_MODULATE)
+            if s < 0:
+                run(transpose, s + AHEAD_MODULATE)
+                run(modulate, s + AHEAD_MODULATE)
             for target, result in waiting_stores:
                 nc.scalar.dma_start(out=target, in_=result[:])
             waiting_stores.clear()

from contextlib import ExitStack

import concourse.mybir as mybir
from concourse.masks import make_identity

F32 = mybir.dt.float32
BF16 = mybir.dt.bfloat16
U32 = mybir.dt.uint32
U8 = mybir.dt.uint8
FP8X4 = mybir.dt.float8_e4m3fn_x4
ACT = mybir.ActivationFunctionType
ALU = mybir.AluOpType

P = 128
PACK = 4
BATCH, TOKENS, DIM = 4, 1024, 512
PROJ, HEADS, HEAD_DIM = 3, 4, 128
PROJ_COLS = HEADS * HEAD_DIM
OUT_COLS = PROJ * PROJ_COLS
QUARTERS = DIM // P
EPS = 1e-5

SPANS = ((2, 2, 2, 2), (2, 2, 4), (4, 4), (4, 4))
CHAIN = 2

AHEAD_STATISTICS = 3
AHEAD_MODULATE = 2
AHEAD_QUANTISE = 1

assert DIM == P * PACK

FLOPS = 2 * BATCH * TOKENS * DIM * OUT_COLS


def tile_localattentionblock_pa_t_kernel(
    tc, x, t_scale, t_shift, ln1_g, ln1_b, qkv_w, qkv_b, out
):
    nc = tc.nc
    regions = []
    chains = []
    for b in range(BATCH):
        first_token = 0
        for span in SPANS[b]:
            regions.append((b, first_token, span))
            for i0 in range(0, span, CHAIN):
                chains.append((b, len(regions) - 1, i0, min(CHAIN, span)))
            first_token += span * P
    n_chains = len(chains)

    with ExitStack() as ctx:
        const = ctx.enter_context(tc.tile_pool(name="const", bufs=1))
        rows = ctx.enter_context(tc.tile_pool(name="rows", bufs=1))
        small = ctx.enter_context(tc.tile_pool(name="small", bufs=8))
        work = ctx.enter_context(tc.tile_pool(name="work", bufs=4))
        results = ctx.enter_context(tc.tile_pool(name="results", bufs=3))
        psum_t = ctx.enter_context(tc.psum_pool(name="psum_t", bufs=1))
        psum_acc = ctx.enter_context(tc.psum_pool(name="psum_acc", bufs=6))
        ctx.enter_context(tc.manual_schedule())

        x_regions = []

        def load_region():
            b, first_token, span = regions[len(x_regions)]
            x_reg = rows.tile([P, span, DIM], BF16, name="x_reg%d" % len(x_regions))
            nc.sync.dma_start(
                out=x_reg[:],
                in_=x[b, first_token : first_token + span * P, :].rearrange(
                    "(p i) k -> p i k", i=span
                ),
            )
            x_regions.append(x_reg)

        w_rows = const.tile([P, PACK, OUT_COLS], BF16)

        def load_weights(j):
            cols = slice(j * PROJ_COLS, (j + 1) * PROJ_COLS)
            nc.sync.dma_start(
                out=w_rows[:, :, cols],
                in_=qkv_w.rearrange("(p t) c -> p t c", t=PACK)[:, :, cols],
            )

        ln_gain = const.tile([P, PACK], BF16)
        ln_shift = const.tile([P, PACK], BF16)
        time_scale = const.tile([P, BATCH, PACK], BF16)
        time_shift = const.tile([P, BATCH, PACK], BF16)
        bias_rows = const.tile([P, OUT_COLS], BF16)

        load_region()
        load_region()
        nc.scalar.dma_start(out=ln_gain[:], in_=ln1_g.rearrange("(p t) -> p t", t=PACK))
        nc.scalar.dma_start(out=ln_shift[:], in_=ln1_b.rearrange("(p t) -> p t", t=PACK))
        nc.sync.dma_start(out=time_scale[:], in_=t_scale.rearrange("b (p t) -> p b t", t=PACK))
        nc.sync.dma_start(out=time_shift[:], in_=t_shift.rearrange("b (p t) -> p b t", t=PACK))
        load_weights(0)
        load_region()
        load_weights(1)
        load_weights(2)
        nc.sync.dma_start(out=bias_rows[:], in_=qkv_b.partition_broadcast(P))
        for r in range(len(x_regions), len(regions)):
            load_region()

        eps = const.tile([P, 1], F32)
        nc.vector.memset(eps[:], EPS)
        warm = const.tile([P, 1], F32)
        nc.scalar.activation(out=warm[:], in_=eps[:], func=ACT.Abs_reciprocal_sqrt)
        ident = const.tile([P, P], F32)
        make_identity(nc, ident[:])
        ident_bf = const.tile([P, P], BF16)
        make_identity(nc, ident_bf[:])

        one_plus = const.tile([P, BATCH, PACK], F32)
        mod_gain = const.tile([P, BATCH, PACK], F32)
        mod_shift = const.tile([P, BATCH, PACK], F32)

        def fold_modulation():
            per_batch = [P, BATCH, PACK]
            nc.vector.tensor_scalar_add(out=one_plus[:], in0=time_scale[:], scalar1=1.0)
            nc.vector.tensor_mul(
                out=mod_gain[:], in0=one_plus[:], in1=ln_gain[:].unsqueeze(1).to_broadcast(per_batch)
            )
            nc.vector.tensor_mul(
                out=mod_shift[:], in0=one_plus[:], in1=ln_shift[:].unsqueeze(1).to_broadcast(per_batch)
            )
            nc.vector.tensor_add(out=mod_shift[:], in0=mod_shift[:], in1=time_shift[:])

        w_grouped = const.tile([P, OUT_COLS, PACK], BF16, align_bytes=64)
        w_words = const.tile([P, OUT_COLS], U32, align_bytes=64)
        w_scales = const.tile([P, OUT_COLS], U8, align_bytes=64)

        def regroup_weights(j):
            cols = slice(j * PROJ_COLS, (j + 1) * PROJ_COLS)
            woven = w_rows[:, :, cols].rearrange("p t c -> p c t")
            if j == PROJ - 1:
                nc.scalar.copy(out=w_grouped[:, cols, :], in_=woven)
            else:
                nc.vector.tensor_copy(out=w_grouped[:, cols, :], in_=woven)

        def quantise_weights(j):
            cols = slice(j * PROJ_COLS, (j + 1) * PROJ_COLS)
            nc.vector.quantize_mx(
                out=w_words[:, cols].bitcast(FP8X4),
                scales=w_scales[:, cols],
                in_=w_grouped[:, cols, :].rearrange("p c t -> p (c t)"),
            )

        neg_means, rstds, xhats, planes_t, planes, grouped, words, scales = (
            {}, {}, {}, {}, {}, {}, {}, {},
        )
        folds = {}

        def fold(c):
            if c == 0:
                return
            b, r, i0, tiles = chains[c]
            folds[c] = psum_acc.tile([P, PROJ_COLS // P, P], F32, name="acc")
            for u in range(QUARTERS):
                nc.tensor.matmul(
                    out=folds[c][:, :tiles, :], lhsT=ident_bf[:],
                    rhs=x_regions[r][:, i0 : i0 + tiles, u * P : (u + 1) * P],
                    start=(u == 0), stop=(u == QUARTERS - 1),
                )

        def statistics(c):
            b, r, i0, tiles = chains[c]
            rstds[c] = small.tile([P, CHAIN], F32, name="rstd")
            if c == 0:
                moments = small.tile([P, CHAIN, 6], F32, name="moments")
                mean_var = small.tile([P, CHAIN, 2], F32, name="mean_var")
                for i in range(tiles):
                    nc.vector.bn_stats(out=moments[:, i, :], in_=x_regions[r][:, i0 + i, :])
                    nc.vector.bn_aggr(out=mean_var[:, i, :], in_=moments[:, i, :])
                neg_means[c] = small.tile([P, CHAIN], F32, name="neg_mean")
                nc.vector.tensor_scalar_mul(
                    out=neg_means[c][:, :tiles], in0=mean_var[:, :tiles, 0], scalar1=-1.0
                )
                nc.scalar.activation(
                    out=rstds[c][:, :tiles], in_=mean_var[:, :tiles, 1],
                    func=ACT.Abs_reciprocal_sqrt, bias=eps[:],
                )
                return
            unread = work.tile([P, CHAIN, DIM], BF16, name="unread")
            neg_mean = small.tile([P, CHAIN], F32, name="neg_mean")
            spread = small.tile([P, CHAIN], F32, name="spread")
            neg_means[c] = neg_mean
            for i in range(tiles):
                nc.scalar.activation(
                    out=unread[:, i, :P], in_=folds[c][:, i, :], func=ACT.Identity,
                    scale=-1.0 / DIM, accum_out=neg_mean[:, i : i + 1],
                )
            for i in range(tiles):
                nc.scalar.activation(
                    out=unread[:, i, :], in_=x_regions[r][:, i0 + i, :], func=ACT.Square,
                    bias=neg_mean[:, i : i + 1], accum_out=spread[:, i : i + 1],
                )
            nc.scalar.activation(
                out=rstds[c][:, :tiles], in_=spread[:, :tiles], func=ACT.Abs_reciprocal_sqrt,
                scale=1.0 / DIM, bias=eps[:],
            )

        def normalise(c):
            b, r, i0, tiles = chains[c]
            xhats[c] = work.tile([P, CHAIN, PACK, P], F32, name="xhat")
            engine = nc.vector if c == 0 else nc.gpsimd
            for i in range(tiles):
                engine.tensor_scalar(
                    out=xhats[c][:, i, :, :],
                    in0=x_regions[r][:, i0 + i, :].rearrange("n (p t) -> n t p", t=PACK),
                    scalar1=neg_means[c][:, i : i + 1], scalar2=rstds[c][:, i : i + 1],
                    op0=ALU.add, op1=ALU.mult,
                )

        def transpose(c):
            tiles = chains[c][3]
            pair = [psum_t.tile([P, 2, CHAIN * P], F32, name="xhat_t%d" % u) for u in range(2)]
            planes_t[c] = [pair[t // 2][:, t % 2, :] for t in range(PACK)]
            for u in range(2):
                for i in range(tiles):
                    for t in (2 * u, 2 * u + 1):
                        nc.tensor.transpose(
                            out=planes_t[c][t][:, i * P : (i + 1) * P], in_=xhats[c][:, i, t, :],
                            identity=ident[:],
                        )

        def modulate(c):
            b, r, i0, tiles = chains[c]
            planes[c] = work.tile([P, PACK, CHAIN * P], BF16, name="planes")
            for t in range(PACK):
                nc.scalar.activation(
                    out=planes[c][:, t, : tiles * P], in_=planes_t[c][t][:, : tiles * P],
                    func=ACT.Identity,
                    scale=mod_gain[:, b, t : t + 1], bias=mod_shift[:, b, t : t + 1],
                )

        def regroup(c):
            tiles = chains[c][3]
            grouped[c] = work.tile([P, CHAIN * P, PACK], BF16, name="grouped", align_bytes=64)
            woven = planes[c][:, :, : tiles * P].rearrange("p t n -> p n t")
            if c == 0:
                nc.vector.tensor_copy(out=grouped[c][:, : tiles * P, :], in_=woven)
            else:
                nc.gpsimd.tensor_scalar(
                    out=grouped[c][:, : tiles * P, :], in0=woven,
                    scalar1=1.0, scalar2=0.0, op0=ALU.mult, op1=ALU.add,
                )

        def quantise(c):
            tiles = chains[c][3]
            words[c] = work.tile([P, CHAIN * P], U32, name="words", align_bytes=64)
            scales[c] = work.tile([P, CHAIN * P], U8, name="scales", align_bytes=64)
            nc.vector.quantize_mx(
                out=words[c][:, : tiles * P].bitcast(FP8X4), scales=scales[c][:, : tiles * P],
                in_=grouped[c][:, : tiles * P, :].rearrange("p n t -> p (n t)"),
            )

        open_results = {}
        waiting_stores = []

        def project(c, j):
            b, r, i0, tiles = chains[c]
            first_token, span = regions[r][1], regions[r][2]
            cols = slice(j * PROJ_COLS, (j + 1) * PROJ_COLS)
            if i0 == 0:
                open_results[j] = results.tile([P, HEADS, span, HEAD_DIM], F32, name="result%d" % j)
            result = open_results[j]
            for i in range(tiles):
                tokens = slice(i * P, (i + 1) * P)
                acc = psum_acc.tile([P, PROJ_COLS], F32, name="acc")
                nc.tensor.matmul_mx(
                    out=acc[:],
                    lhsT=words[c][:, tokens].bitcast(FP8X4), lhsT_scale=scales[c][:, tokens],
                    rhs=w_words[:, cols].bitcast(FP8X4), rhs_scale=w_scales[:, cols],
                    start=True, stop=True,
                )
                nc.vector.tensor_tensor(
                    out=result[:, :, i0 + i, :],
                    in0=acc[:].rearrange("p (h d) -> p h d", h=HEADS),
                    in1=bias_rows[:, cols].rearrange("p (h d) -> p h d", h=HEADS),
                    op=ALU.add,
                )
            if i0 + tiles == span:
                target = out[j, b, :, first_token : first_token + span * P, :].rearrange(
                    "h (p i) d -> p h i d", i=span
                )
                if j == 1 and c < n_chains - 1:
                    waiting_stores.append((target, result))
                else:
                    nc.sync.dma_start(out=target, in_=result[:])

        def run(stage, c):
            if 0 <= c < n_chains:
                stage(c)

        for s in range(-AHEAD_STATISTICS, n_chains):
            if s >= 0:
                project(s, 0)
            if s == 0:
                quantise_weights(2)
            run(fold, s + AHEAD_STATISTICS)
            run(statistics, s + AHEAD_STATISTICS)
            if s == -AHEAD_STATISTICS:
                fold_modulation()
            run(regroup, s + AHEAD_QUANTISE)
            if s >= 0:
                project(s, 1)
            run(quantise, s + AHEAD_QUANTISE)
            if s == -1:
                regroup_weights(1)
                regroup_weights(2)
                quantise_weights(1)
            if s >= 0:
                run(transpose, s + AHEAD_MODULATE)
                run(modulate, s + AHEAD_MODULATE)
                project(s, 2)
            run(normalise, s + AHEAD_STATISTICS)
            if s == -AHEAD_MODULATE:
                regroup_weights(0)
                quantise_weights(0)
            if s < 0:
                run(transpose, s + AHEAD_MODULATE)
                run(modulate, s + AHEAD_MODULATE)
            for target, result in waiting_stores:
                nc.scalar.dma_start(out=target, in_=result[:])
            waiting_stores.clear()
